import numpy as np
import ml_dtypes


def mxq(x, axis, fmt="e4m3"):
    dtype, down = {"e4m3": (ml_dtypes.float8_e4m3fn, 7), "e5m2": (ml_dtypes.float8_e5m2, 14)}[fmt]
    v = np.moveaxis(np.asarray(x, np.float32).astype(ml_dtypes.bfloat16).astype(np.float64), axis, -1)
    blocks = v.reshape(v.shape[:-1] + (-1, 32))
    amax = np.abs(blocks).max(-1, keepdims=True)
    byte = np.maximum(np.where(amax > 0, np.frexp(amax)[1] - 1 + 127, 0) - down, 1)
    scale = np.exp2(byte - 127.0)
    codes = (blocks / scale).astype(np.float32).astype(dtype).astype(np.float64)
    return np.moveaxis((codes * scale).reshape(v.shape), -1, axis)


WIDE = False


def mx_kscale(k):
    if not WIDE:
        return np.ones(k)
    levels = np.array([10, -10, 5, -5, 0])
    a = np.random.permutation(np.resize(levels, k // 512 * 4)).reshape(k // 512, 4)
    idx = np.arange(k)
    return np.exp2(a[idx // 512, idx % 128 // 32])


BF16 = ml_dtypes.bfloat16


def bf(x):
    return np.asarray(x, np.float32).astype(BF16)


def f64(x):
    return np.asarray(x).astype(np.float64)


B, C, V, K, OUT = 4, 128, 2048, 4, 128


def setup_inputs():
    a = mx_kscale(C * K)[::K]
    ab = np.repeat(a, B)
    ak = np.repeat(a, K)
    g = np.random.standard_normal((V, V))
    lap = (g + g.T) * (0.45 / np.sqrt(V))
    return {"input": bf(np.random.standard_normal((B, C, V)) * a[None, :, None]),
            "x1": bf(np.random.standard_normal((V, C * B)) * 0.64 * ab),
            "x2": bf(np.random.standard_normal((V, C * B)) * 0.83 * ab),
            "laplacian": bf(lap),
            "weight": bf(np.random.standard_normal((OUT, C * K)) / np.sqrt(C * K) / ak),
            "bias": bf(np.random.standard_normal(OUT) * 0.2)}


def reference(input, x1, x2, laplacian, weight, bias):
    x0 = f64(input).transpose(2, 1, 0).reshape(V, C * B)
    x1 = f64(x1)
    x2 = f64(x2)
    x3 = 2.0 * (mxq(f64(laplacian), 1, "e4m3") @ mxq(x2, 0, "e4m3")) - x1
    x = np.stack([x0, x1, x2, x3], axis=0)
    x = x.reshape(K, V, C, B)
    x = x.transpose(3, 1, 2, 0)
    x = x.reshape(B * V, C * K)
    y = (mxq(x, 1, "e4m3") @ mxq(f64(weight), 1, "e4m3").T) + f64(bias)
    y = y.reshape(B, V, OUT)
    return y.transpose(0, 2, 1)

@@ -1,0 +1,267 @@
+from contextlib import ExitStack
+
+import concourse.mybir as mybir
+from concourse.masks import make_identity
+
+BF16 = mybir.dt.bfloat16
+F32 = mybir.dt.float32
+U32 = mybir.dt.uint32
+U8 = mybir.dt.uint8
+FP8X4 = mybir.dt.float8_e4m3fn_x4
+
+P = 128
+PACK = 4
+K_PASS = P * PACK
+N_TILE = 512
+
+B, C, V, ORDERS, OUT = 4, 128, 2048, 4, 128
+CB = C * B
+CHUNKS = V // N_TILE
+PASSES = V // K_PASS
+UNITS = CHUNKS * B
+LAP_PASSES = CHUNKS * PASSES
+LEAD = 5
+SCALAR_COLS = 128
+
+FLOPS = 2 * V * V * CB + 2 * B * V * C * ORDERS * OUT
+
+
+def tile_graph_conv_pb_kernel(tc, x0_dram, x1_dram, x2_dram, lap_dram, w_dram, bias_dram, out_dram):
+    nc = tc.nc
+    mult = mybir.AluOpType.mult
+    subtract = mybir.AluOpType.subtract
+
+    with ExitStack() as ctx:
+        keep = ctx.enter_context(tc.tile_pool(name="keep", bufs=1))
+        two = ctx.enter_context(tc.tile_pool(name="two", bufs=2))
+        three = ctx.enter_context(tc.tile_pool(name="three", bufs=3))
+        flip_psum = ctx.enter_context(tc.psum_pool(name="flip", bufs=4))
+        acc_psum = ctx.enter_context(tc.psum_pool(name="acc", bufs=2))
+        y_psum = ctx.enter_context(tc.psum_pool(name="y", bufs=2))
+
+        ident = keep.tile([P, P], F32)
+        make_identity(nc, ident[:])
+        bias_square = keep.tile([P, P], F32)
+        nc.vector.memset(bias_square[:], 0.0)
+
+        w_rows = keep.tile([OUT, C * ORDERS], BF16)
+        nc.sync.dma_start(out=w_rows[:], in_=w_dram)
+        bias_row = keep.tile([1, OUT], BF16)
+        nc.sync.dma_start(out=bias_row[:], in_=bias_dram.rearrange("(one o) -> one o", one=1))
+
+        term_rows = {}
+        for name, dram in (("x2", x2_dram), ("x1", x1_dram)):
+            rows = keep.tile([P, PASSES * PACK * CB], BF16, name=name + "_rows")
+            view = dram.rearrange("(g uh q e) w -> g q uh (e w)", g=PASSES, uh=2, q=P, e=2)
+            for g in range(PASSES):
+                nc.sync.dma_start(
+                    out=rows[:, g * PACK * CB : (g + 1) * PACK * CB].rearrange("q (uh r) -> q uh r", uh=2),
+                    in_=view[g],
+                )
+            term_rows[name] = rows
+
+        lap_view = lap_dram.rearrange("(i p j) u -> i p (j u)", i=CHUNKS, p=P, j=PACK)
+        lap_rows = {}
+
+        def load_lap_chunk(i):
+            rows = two.tile([P, PACK * V], BF16, name="lap_rows")
+            half = PACK * V // 2
+            for a in range(2):
+                nc.sync.dma_start(out=rows[:, a * half : (a + 1) * half], in_=lap_view[i][:, a * half : (a + 1) * half])
+            lap_rows[i] = rows
+
+        x0_view = x0_dram.rearrange("b c v -> c b v")
+        planes = {}
+
+        def load_x0_chunk(i):
+            chunk_planes = keep.tile([P, ORDERS, B, N_TILE], BF16, name="planes%d" % i)
+            nc.sync.dma_start(out=chunk_planes[:, 0, :, :], in_=x0_view[:, :, i * N_TILE : (i + 1) * N_TILE])
+            planes[i] = chunk_planes
+
+        load_lap_chunk(0)
+        load_x0_chunk(0)
+        load_lap_chunk(1)
+        load_x0_chunk(1)
+        load_x0_chunk(2)
+        load_x0_chunk(3)
+        load_lap_chunk(2)
+        load_lap_chunk(3)
+
+        w_words = w_rows[:].bitcast(F32).rearrange("o (c hh) -> o hh c", hh=2)
+        w_flip = flip_psum.tile([P, N_TILE], F32, name="flip")
+        for hh in range(2):
+            nc.tensor.transpose(w_flip[:, hh * OUT : (hh + 1) * OUT], w_words[:, hh, :], ident[:])
+        w_grouped = keep.tile([P, OUT * PACK], BF16, align_bytes=64)
+        nc.vector.tensor_copy(
+            out=w_grouped[:].bitcast(F32).rearrange("c (o hh) -> c o hh", hh=2),
+            in_=w_flip[:, 0 : 2 * OUT].rearrange("c (hh o) -> c o hh", hh=2),
+        )
+        w_codes = keep.tile([P, OUT], U32, align_bytes=64)
+        w_scales = keep.tile([P, OUT], U8, align_bytes=64)
+        nc.vector.quantize_mx(out=w_codes[:].bitcast(FP8X4), scales=w_scales[:], in_=w_grouped[:])
+
+        nc.vector.tensor_copy(out=bias_square[0:1, :], in_=bias_row[:])
+        bias_flip = flip_psum.tile([P, N_TILE], F32, name="flip")
+        nc.tensor.transpose(bias_flip[:, 0:P], bias_square[:], ident[:])
+        bias_col = keep.tile([P, 1], F32)
+        nc.vector.tensor_copy(out=bias_col[:], in_=bias_flip[:, 0:1])
+
+        x2_codes = keep.tile([P, PASSES, CB], U32, align_bytes=64)
+        x2_scales = keep.tile([P, PASSES, CB], U8, align_bytes=64)
+        x2_grouped = {}
+        for g in range(PASSES + 1):
+            if g < PASSES:
+                grouped = two.tile([P, CB * PACK], BF16, align_bytes=64, name="x2_grouped")
+                nc.vector.tensor_copy(
+                    out=grouped[:].rearrange("q (b c t) -> q b c t", b=B, c=C),
+                    in_=term_rows["x2"][:, g * PACK * CB : (g + 1) * PACK * CB].rearrange(
+                        "q (t c b) -> q b c t", t=PACK, c=C
+                    ),
+                )
+                x2_grouped[g] = grouped
+            if g > 0:
+                nc.vector.quantize_mx(
+                    out=x2_codes[:, g - 1, :].bitcast(FP8X4), scales=x2_scales[:, g - 1, :], in_=x2_grouped[g - 1][:]
+                )
+
+        def transpose_term(name, order, g, h, copy):
+            words = term_rows[name][:].bitcast(F32).rearrange(
+                "q (g t c h) -> q g t h c", g=PASSES, t=PACK, c=C
+            )
+            flip = flip_psum.tile([P, N_TILE], F32, name="flip")
+            for e in range(2):
+                for uh in range(2):
+                    slot = e * 2 + uh
+                    nc.tensor.transpose(flip[:, slot * P : (slot + 1) * P], words[:, g, 2 * uh + e, h, :], ident[:])
+            copy(
+                out=planes[g][:, order, 2 * h : 2 * h + 2, :].rearrange("c eb (n e) -> c eb n e", e=2),
+                in_=flip[:].bitcast(BF16).rearrange("c (e n eb) -> c eb n e", e=2, eb=2),
+            )
+
+        for g in range(PASSES):
+            for h in range(2):
+                transpose_term("x2", 2, g, h, nc.scalar.copy)
+        for g in range(PASSES):
+            transpose_term("x1", 1, g, 0, nc.scalar.copy)
+            transpose_term("x1", 1, g, 1, nc.vector.tensor_copy)
+
+        lap_grouped = {}
+        lap_codes = {}
+        lap_scales = {}
+
+        def transpose_lap_piece(piece):
+            i, g = divmod(piece, PASSES)
+            words = lap_rows[i][:].bitcast(F32).rearrange("p (j w) -> p j w", j=PACK)
+            grouped = three.tile([P, N_TILE * PACK], BF16, align_bytes=64, name="lap_grouped")
+            grouped_words = grouped[:].bitcast(F32).rearrange("q (n uh) -> q n uh", uh=2)
+            for a in range(2):
+                flip = flip_psum.tile([P, N_TILE], F32, name="flip")
+                for jl in range(2):
+                    for uh in range(2):
+                        slot = jl * 2 + uh
+                        first = (K_PASS // 2) * g + P * uh
+                        nc.tensor.transpose(
+                            flip[:, slot * P : (slot + 1) * P], words[:, 2 * a + jl, first : first + P], ident[:]
+                        )
+                nc.scalar.copy(
+                    out=grouped_words[:, 2 * P * a : 2 * P * (a + 1), :].rearrange("q (jl p) uh -> q jl p uh", jl=2),
+                    in_=flip[:].rearrange("q (jl uh p) -> q jl p uh", jl=2, uh=2),
+                )
+            lap_grouped[piece] = grouped
+
+        def quantise_lap_piece(piece):
+            i, g = divmod(piece, PASSES)
+            if g == 0:
+                lap_codes[i] = two.tile([P, PASSES, N_TILE], U32, align_bytes=64, name="lap_codes")
+                lap_scales[i] = two.tile([P, PASSES, N_TILE], U8, align_bytes=64, name="lap_scales")
+            nc.vector.quantize_mx(
+                out=lap_codes[i][:, g, :].bitcast(FP8X4), scales=lap_scales[i][:, g, :], in_=lap_grouped[piece][:]
+            )
+
+        acc = {}
+        feat_codes = {}
+        feat_scales = {}
+        feat = {}
+
+        def first_matmul(unit):
+            i, b = divmod(unit, B)
+            acc[unit] = acc_psum.tile([P, N_TILE], F32, name="acc")
+            for g in range(PASSES):
+                nc.tensor.matmul_mx(
+                    out=acc[unit][:],
+                    lhsT=x2_codes[:, g, b * C : (b + 1) * C].bitcast(FP8X4),
+                    lhsT_scale=x2_scales[:, g, b * C : (b + 1) * C],
+                    rhs=lap_codes[i][:, g, :].bitcast(FP8X4),
+                    rhs_scale=lap_scales[i][:, g, :],
+                    start=(g == 0),
+                    stop=(g == PASSES - 1),
+                )
+
+        def third_term(unit):
+            i, b = divmod(unit, B)
+            nc.vector.scalar_tensor_tensor(
+                out=planes[i][:, 3, b, :].rearrange("c (p j) -> c p j", j=PACK),
+                in0=acc[unit][:].rearrange("c (j p) -> c p j", j=PACK),
+                scalar=2.0,
+                in1=planes[i][:, 1, b, :].rearrange("c (p j) -> c p j", j=PACK),
+                op0=mult,
+                op1=subtract,
+            )
+
+        def interleave_features(unit):
+            i, b = divmod(unit, B)
+            feat[unit] = three.tile([P, N_TILE, ORDERS], BF16, align_bytes=64, name="feat")
+            split = N_TILE - SCALAR_COLS
+            for copy, cols in ((nc.vector.tensor_copy, slice(0, split)), (nc.scalar.copy, slice(split, N_TILE))):
+                copy(
+                    out=feat[unit][:, cols, :].rearrange("c (n r) k -> c n k r", r=4),
+                    in_=planes[i][:, :, b, cols].rearrange("c k (n r) -> c n k r", r=4),
+                )
+
+        def quantise_features(unit):
+            feat_codes[unit] = three.tile([P, N_TILE], U32, align_bytes=64, name="feat_codes")
+            feat_scales[unit] = three.tile([P, N_TILE], U8, align_bytes=64, name="feat_scales")
+            nc.vector.quantize_mx(
+                out=feat_codes[unit][:].bitcast(FP8X4),
+                scales=feat_scales[unit][:],
+                in_=feat[unit][:].rearrange("c n k -> c (n k)"),
+            )
+
+        def second_matmul(unit):
+            i, b = divmod(unit, B)
+            y = y_psum.tile([P, N_TILE], F32)
+            nc.tensor.matmul_mx(
+                out=y[:],
+                lhsT=w_codes[:].bitcast(FP8X4),
+                lhsT_scale=w_scales[:],
+                rhs=feat_codes[unit][:].bitcast(FP8X4),
+                rhs_scale=feat_scales[unit][:],
+                start=True,
+                stop=True,
+            )
+            y_sb = three.tile([P, N_TILE], F32)
+            nc.scalar.activation(
+                out=y_sb[:], in_=y[:], func=mybir.ActivationFunctionType.Identity, bias=bias_col[:, 0:1], scale=1.0
+            )
+            nc.scalar.dma_start(out=out_dram[b, :, i * N_TILE : (i + 1) * N_TILE], in_=y_sb[:])
+
+        for piece in range(PASSES + 1):
+            if piece < PASSES:
+                transpose_lap_piece(piece)
+            if piece > 0:
+                quantise_lap_piece(piece - 1)
+        transposed = PASSES
+
+        for unit in range(UNITS):
+            first_matmul(unit)
+            if unit > 0:
+                second_matmul(unit - 1)
+            third_term(unit)
+            interleave_features(unit)
+            while transposed < min(unit + LEAD + 1, LAP_PASSES):
+                transpose_lap_piece(transposed)
+                transposed += 1
+            if unit + PASSES < LAP_PASSES:
+                quantise_lap_piece(unit + PASSES)
+            quantise_features(unit)
+        second_matmul(UNITS - 1)

@@ -38,6 +38,7 @@ def tile_graph_conv_pb_kernel(tc, x0_dram, x1_dram, x2_dram, lap_dram, w_dram, b
         flip_psum = ctx.enter_context(tc.psum_pool(name="flip", bufs=4))
         acc_psum = ctx.enter_context(tc.psum_pool(name="acc", bufs=2))
         y_psum = ctx.enter_context(tc.psum_pool(name="y", bufs=2))
+        ctx.enter_context(tc.manual_schedule())
 
         ident = keep.tile([P, P], F32)
         make_identity(nc, ident[:])

@@ -21,7 +21,7 @@ PASSES = V // K_PASS
 UNITS = CHUNKS * B
 LAP_PASSES = CHUNKS * PASSES
 LEAD = 5
-SCALAR_COLS = 128
+SCALAR_COLS = 64
 
 FLOPS = 2 * V * V * CB + 2 * B * V * C * ORDERS * OUT
 
@@ -50,16 +50,20 @@ def tile_graph_conv_pb_kernel(tc, x0_dram, x1_dram, x2_dram, lap_dram, w_dram, b
         bias_row = keep.tile([1, OUT], BF16)
         nc.sync.dma_start(out=bias_row[:], in_=bias_dram.rearrange("(one o) -> one o", one=1))
 
-        term_rows = {}
-        for name, dram in (("x2", x2_dram), ("x1", x1_dram)):
-            rows = keep.tile([P, PASSES * PACK * CB], BF16, name=name + "_rows")
-            view = dram.rearrange("(g uh q e) w -> g q uh (e w)", g=PASSES, uh=2, q=P, e=2)
-            for g in range(PASSES):
-                nc.sync.dma_start(
-                    out=rows[:, g * PACK * CB : (g + 1) * PACK * CB].rearrange("q (uh r) -> q uh r", uh=2),
-                    in_=view[g],
-                )
-            term_rows[name] = rows
+        term_rows = {
+            "x1": keep.tile([P, PASSES * PACK * CB], BF16, name="x1_rows"),
+            "x2": keep.tile([P, PASSES * PACK * CB], BF16, name="x2_rows"),
+        }
+        term_views = {
+            "x1": x1_dram.rearrange("(g uh q e) w -> g q uh (e w)", g=PASSES, uh=2, q=P, e=2),
+            "x2": x2_dram.rearrange("(g uh q e) w -> g q uh (e w)", g=PASSES, uh=2, q=P, e=2),
+        }
+
+        def load_term_piece(name, g):
+            nc.sync.dma_start(
+                out=term_rows[name][:, g * PACK * CB : (g + 1) * PACK * CB].rearrange("q (uh r) -> q uh r", uh=2),
+                in_=term_views[name][g],
+            )
 
         lap_view = lap_dram.rearrange("(i p j) u -> i p (j u)", i=CHUNKS, p=P, j=PACK)
         lap_rows = {}
@@ -79,12 +83,15 @@ def tile_graph_conv_pb_kernel(tc, x0_dram, x1_dram, x2_dram, lap_dram, w_dram, b
             nc.sync.dma_start(out=chunk_planes[:, 0, :, :], in_=x0_view[:, :, i * N_TILE : (i + 1) * N_TILE])
             planes[i] = chunk_planes
 
+        for g in range(PASSES):
+            load_term_piece("x2", g)
         load_lap_chunk(0)
+        load_term_piece("x1", 0)
         load_x0_chunk(0)
         load_lap_chunk(1)
-        load_x0_chunk(1)
-        load_x0_chunk(2)
-        load_x0_chunk(3)
+        for i in range(1, CHUNKS):
+            load_term_piece("x1", i)
+            load_x0_chunk(i)
         load_lap_chunk(2)
         load_lap_chunk(3)
 
@@ -142,15 +149,12 @@ def tile_graph_conv_pb_kernel(tc, x0_dram, x1_dram, x2_dram, lap_dram, w_dram, b
         for g in range(PASSES):
             for h in range(2):
                 transpose_term("x2", 2, g, h, nc.scalar.copy)
-        for g in range(PASSES):
-            transpose_term("x1", 1, g, 0, nc.scalar.copy)
-            transpose_term("x1", 1, g, 1, nc.vector.tensor_copy)
 
         lap_grouped = {}
         lap_codes = {}
         lap_scales = {}
 
-        def transpose_lap_piece(piece):
+        def transpose_lap_piece(piece, second_copy):
             i, g = divmod(piece, PASSES)
             words = lap_rows[i][:].bitcast(F32).rearrange("p (j w) -> p j w", j=PACK)
             grouped = three.tile([P, N_TILE * PACK], BF16, align_bytes=64, name="lap_grouped")
@@ -164,7 +168,8 @@ def tile_graph_conv_pb_kernel(tc, x0_dram, x1_dram, x2_dram, lap_dram, w_dram, b
                         nc.tensor.transpose(
                             flip[:, slot * P : (slot + 1) * P], words[:, 2 * a + jl, first : first + P], ident[:]
                         )
-                nc.scalar.copy(
+                copy = (nc.scalar.copy, second_copy)[a]
+                copy(
                     out=grouped_words[:, 2 * P * a : 2 * P * (a + 1), :].rearrange("q (jl p) uh -> q jl p uh", jl=2),
                     in_=flip[:].rearrange("q (jl uh p) -> q jl p uh", jl=2, uh=2),
                 )
@@ -209,15 +214,12 @@ def tile_graph_conv_pb_kernel(tc, x0_dram, x1_dram, x2_dram, lap_dram, w_dram, b
                 op1=subtract,
             )
 
-        def interleave_features(unit):
+        def interleave_features(unit, copy, cols):
             i, b = divmod(unit, B)
-            feat[unit] = three.tile([P, N_TILE, ORDERS], BF16, align_bytes=64, name="feat")
-            split = N_TILE - SCALAR_COLS
-            for copy, cols in ((nc.vector.tensor_copy, slice(0, split)), (nc.scalar.copy, slice(split, N_TILE))):
-                copy(
-                    out=feat[unit][:, cols, :].rearrange("c (n r) k -> c n k r", r=4),
-                    in_=planes[i][:, :, b, cols].rearrange("c k (n r) -> c n k r", r=4),
-                )
+            copy(
+                out=feat[unit][:, cols, :].rearrange("c (n r) k -> c n k r", r=4),
+                in_=planes[i][:, :, b, cols].rearrange("c k (n r) -> c n k r", r=4),
+            )
 
         def quantise_features(unit):
             feat_codes[unit] = three.tile([P, N_TILE], U32, align_bytes=64, name="feat_codes")
@@ -248,21 +250,31 @@ def tile_graph_conv_pb_kernel(tc, x0_dram, x1_dram, x2_dram, lap_dram, w_dram, b
 
         for piece in range(PASSES + 1):
             if piece < PASSES:
-                transpose_lap_piece(piece)
+                transpose_lap_piece(piece, nc.vector.tensor_copy)
             if piece > 0:
                 quantise_lap_piece(piece - 1)
         transposed = PASSES
+        transpose_term("x1", 1, 0, 0, nc.scalar.copy)
+        transpose_term("x1", 1, 0, 1, nc.vector.tensor_copy)
 
-        for unit in range(UNITS):
-            first_matmul(unit)
-            if unit > 0:
-                second_matmul(unit - 1)
-            third_term(unit)
-            interleave_features(unit)
+        first_matmul(0)
+        for unit in range(UNITS + 1):
+            i, b = divmod(unit, B)
+            if unit < UNITS:
+                third_term(unit)
+                feat[unit] = three.tile([P, N_TILE, ORDERS], BF16, align_bytes=64, name="feat")
+                interleave_features(unit, nc.scalar.copy, slice(N_TILE - SCALAR_COLS, N_TILE))
             while transposed < min(unit + LEAD + 1, LAP_PASSES):
-                transpose_lap_piece(transposed)
+                transpose_lap_piece(transposed, nc.scalar.copy)
                 transposed += 1
+            if i + 1 < CHUNKS and b % 2 == 0:
+                transpose_term("x1", 1, i + 1, b // 2, nc.scalar.copy)
             if unit + PASSES < LAP_PASSES:
                 quantise_lap_piece(unit + PASSES)
-            quantise_features(unit)
-        second_matmul(UNITS - 1)
+            if unit + 1 < UNITS:
+                first_matmul(unit + 1)
+            if unit > 0:
+                quantise_features(unit - 1)
+                second_matmul(unit - 1)
+            if unit < UNITS:
+                interleave_features(unit, nc.vector.tensor_copy, slice(0, N_TILE - SCALAR_COLS))

@@ -42,6 +42,8 @@ def tile_graph_conv_pb_kernel(tc, x0_dram, x1_dram, x2_dram, lap_dram, w_dram, b
 
         ident = keep.tile([P, P], F32)
         make_identity(nc, ident[:])
+        ident_half = keep.tile([P, P], BF16)
+        nc.vector.tensor_copy(out=ident_half[:], in_=ident[:])
         bias_square = keep.tile([P, P], F32)
         nc.vector.memset(bias_square[:], 0.0)
 
@@ -55,13 +57,15 @@ def tile_graph_conv_pb_kernel(tc, x0_dram, x1_dram, x2_dram, lap_dram, w_dram, b
             "x2": keep.tile([P, PASSES * PACK * CB], BF16, name="x2_rows"),
         }
         term_views = {
-            "x1": x1_dram.rearrange("(g uh q e) w -> g q uh (e w)", g=PASSES, uh=2, q=P, e=2),
+            "x1": x1_dram.rearrange("(g s q) w -> g q s w", g=PASSES, s=PACK, q=P),
             "x2": x2_dram.rearrange("(g uh q e) w -> g q uh (e w)", g=PASSES, uh=2, q=P, e=2),
         }
 
         def load_term_piece(name, g):
             nc.sync.dma_start(
-                out=term_rows[name][:, g * PACK * CB : (g + 1) * PACK * CB].rearrange("q (uh r) -> q uh r", uh=2),
+                out=term_rows[name][:, g * PACK * CB : (g + 1) * PACK * CB].rearrange(
+                    "q (s r) -> q s r", s=term_views[name].shape[2]
+                ),
                 in_=term_views[name][g],
             )
 
@@ -145,6 +149,17 @@ def tile_graph_conv_pb_kernel(tc, x0_dram, x1_dram, x2_dram, lap_dram, w_dram, b
                 out=planes[g][:, order, 2 * h : 2 * h + 2, :].rearrange("c eb (n e) -> c eb n e", e=2),
                 in_=flip[:].bitcast(BF16).rearrange("c (e n eb) -> c eb n e", e=2, eb=2),
             )
+
+        def transpose_x1(g, h, copy):
+            values = term_rows["x1"][:].rearrange("q (g s c b) -> q g s b c", g=PASSES, s=PACK, c=C)
+            flip = flip_psum.tile([P, 2 * N_TILE], BF16, name="flip")
+            for eb in range(2):
+                for s in range(PACK):
+                    slot = eb * PACK + s
+                    nc.tensor.transpose(
+                        flip[:, slot * P : (slot + 1) * P], values[:, g, s, 2 * h + eb, :], ident_half[:]
+                    )
+            copy(out=planes[g][:, 1, 2 * h : 2 * h + 2, :].rearrange("c eb v -> c (eb v)"), in_=flip[:])
 
         for g in range(PASSES):
             for h in range(2):
@@ -254,8 +269,8 @@ def tile_graph_conv_pb_kernel(tc, x0_dram, x1_dram, x2_dram, lap_dram, w_dram, b
             if piece > 0:
                 quantise_lap_piece(piece - 1)
         transposed = PASSES
-        transpose_term("x1", 1, 0, 0, nc.scalar.copy)
-        transpose_term("x1", 1, 0, 1, nc.vector.tensor_copy)
+        transpose_x1(0, 0, nc.scalar.copy)
+        transpose_x1(0, 1, nc.vector.tensor_copy)
 
         first_matmul(0)
         for unit in range(UNITS + 1):
@@ -268,7 +283,7 @@ def tile_graph_conv_pb_kernel(tc, x0_dram, x1_dram, x2_dram, lap_dram, w_dram, b
                 transpose_lap_piece(transposed, nc.scalar.copy)
                 transposed += 1
             if i + 1 < CHUNKS and b % 2 == 0:
-                transpose_term("x1", 1, i + 1, b // 2, nc.scalar.copy)
+                transpose_x1(i + 1, b // 2, nc.scalar.copy)
             if unit + PASSES < LAP_PASSES:
                 quantise_lap_piece(unit + PASSES)
             if unit + 1 < UNITS:

@@ -20,8 +20,9 @@ CHUNKS = V // N_TILE
 PASSES = V // K_PASS
 UNITS = CHUNKS * B
 LAP_PASSES = CHUNKS * PASSES
-LEAD = 5
-SCALAR_COLS = 64
+LEAD = 6
+SCALAR_COLS = 128
+SCALAR_COLS_END = 192
 
 FLOPS = 2 * V * V * CB + 2 * B * V * C * ORDERS * OUT
 
@@ -34,6 +35,7 @@ def tile_graph_conv_pb_kernel(tc, x0_dram, x1_dram, x2_dram, lap_dram, w_dram, b
     with ExitStack() as ctx:
         keep = ctx.enter_context(tc.tile_pool(name="keep", bufs=1))
         two = ctx.enter_context(tc.tile_pool(name="two", bufs=2))
+        four = ctx.enter_context(tc.tile_pool(name="four", bufs=4))
         three = ctx.enter_context(tc.tile_pool(name="three", bufs=3))
         flip_psum = ctx.enter_context(tc.psum_pool(name="flip", bufs=4))
         acc_psum = ctx.enter_context(tc.psum_pool(name="acc", bufs=2))
@@ -47,148 +49,138 @@ def tile_graph_conv_pb_kernel(tc, x0_dram, x1_dram, x2_dram, lap_dram, w_dram, b
         bias_square = keep.tile([P, P], F32)
         nc.vector.memset(bias_square[:], 0.0)
 
-        w_rows = keep.tile([OUT, C * ORDERS], BF16)
-        nc.sync.dma_start(out=w_rows[:], in_=w_dram)
-        bias_row = keep.tile([1, OUT], BF16)
-        nc.sync.dma_start(out=bias_row[:], in_=bias_dram.rearrange("(one o) -> one o", one=1))
-
         term_rows = {
-            "x1": keep.tile([P, PASSES * PACK * CB], BF16, name="x1_rows"),
-            "x2": keep.tile([P, PASSES * PACK * CB], BF16, name="x2_rows"),
+            "x1": keep.tile([P, CHUNKS * PACK * CB], BF16, name="x1_rows"),
+            "x2": keep.tile([P, CHUNKS * PACK * CB], BF16, name="x2_rows"),
         }
         term_views = {
-            "x1": x1_dram.rearrange("(g s q) w -> g q s w", g=PASSES, s=PACK, q=P),
-            "x2": x2_dram.rearrange("(g uh q e) w -> g q uh (e w)", g=PASSES, uh=2, q=P, e=2),
+            "x1": x1_dram.rearrange("(g s q) w -> g q s w", g=CHUNKS, s=PACK, q=P),
+            "x2": x2_dram.rearrange("(g s q) w -> g q s w", g=CHUNKS, s=PACK, q=P),
         }
 
-        def load_term_piece(name, g):
-            nc.sync.dma_start(
-                out=term_rows[name][:, g * PACK * CB : (g + 1) * PACK * CB].rearrange(
-                    "q (s r) -> q s r", s=term_views[name].shape[2]
-                ),
-                in_=term_views[name][g],
-            )
+        def load_term_chunk(name, g, slots=slice(0, PACK)):
+            rows = term_rows[name][:, g * PACK * CB : (g + 1) * PACK * CB].rearrange("q (s w) -> q s w", s=PACK)
+            nc.sync.dma_start(out=rows[:, slots, :], in_=term_views[name][g][:, slots, :])
 
-        lap_view = lap_dram.rearrange("(i p j) u -> i p (j u)", i=CHUNKS, p=P, j=PACK)
+        lap_view = lap_dram.rearrange("(i p j) u -> i p j u", i=CHUNKS, p=P, j=PACK)
         lap_rows = {}
 
-        def load_lap_chunk(i):
-            rows = two.tile([P, PACK * V], BF16, name="lap_rows")
-            half = PACK * V // 2
-            for a in range(2):
-                nc.sync.dma_start(out=rows[:, a * half : (a + 1) * half], in_=lap_view[i][:, a * half : (a + 1) * half])
-            lap_rows[i] = rows
+        def load_lap_half(i, a):
+            if a == 0:
+                lap_rows[i] = three.tile([P, PACK, V], BF16, name="lap_rows")
+            half = slice(a * V // 2, (a + 1) * V // 2)
+            nc.sync.dma_start(out=lap_rows[i][:, :, half], in_=lap_view[i][:, :, half])
 
         x0_view = x0_dram.rearrange("b c v -> c b v")
         planes = {}
 
+        for i in range(CHUNKS):
+            planes[i] = keep.tile([P, ORDERS, B, N_TILE], BF16, name="planes%d" % i)
+
         def load_x0_chunk(i):
-            chunk_planes = keep.tile([P, ORDERS, B, N_TILE], BF16, name="planes%d" % i)
-            nc.sync.dma_start(out=chunk_planes[:, 0, :, :], in_=x0_view[:, :, i * N_TILE : (i + 1) * N_TILE])
-            planes[i] = chunk_planes
+            nc.sync.dma_start(out=planes[i][:, 0, :, :], in_=x0_view[:, :, i * N_TILE : (i + 1) * N_TILE])
 
-        for g in range(PASSES):
-            load_term_piece("x2", g)
-        load_lap_chunk(0)
-        load_term_piece("x1", 0)
+        w_rows = keep.tile([OUT, C * ORDERS], BF16)
+        bias_row = keep.tile([1, OUT], BF16)
+        load_term_chunk("x2", 0, slice(0, 2))
+        load_term_chunk("x2", 0, slice(2, PACK))
+        for g in range(1, PASSES):
+            load_term_chunk("x2", g)
+        load_lap_half(0, 0)
+        load_lap_half(0, 1)
+        load_term_chunk("x1", 0)
+        nc.sync.dma_start(out=bias_row[:], in_=bias_dram.rearrange("(one o) -> one o", one=1))
+        nc.sync.dma_start(out=w_rows[:], in_=w_dram)
         load_x0_chunk(0)
-        load_lap_chunk(1)
         for i in range(1, CHUNKS):
-            load_term_piece("x1", i)
+            load_lap_half(i, 0)
+            load_lap_half(i, 1)
+            load_term_chunk("x1", i)
             load_x0_chunk(i)
-        load_lap_chunk(2)
-        load_lap_chunk(3)
 
-        w_words = w_rows[:].bitcast(F32).rearrange("o (c hh) -> o hh c", hh=2)
-        w_flip = flip_psum.tile([P, N_TILE], F32, name="flip")
-        for hh in range(2):
-            nc.tensor.transpose(w_flip[:, hh * OUT : (hh + 1) * OUT], w_words[:, hh, :], ident[:])
-        w_grouped = keep.tile([P, OUT * PACK], BF16, align_bytes=64)
-        nc.vector.tensor_copy(
-            out=w_grouped[:].bitcast(F32).rearrange("c (o hh) -> c o hh", hh=2),
-            in_=w_flip[:, 0 : 2 * OUT].rearrange("c (hh o) -> c o hh", hh=2),
-        )
         w_codes = keep.tile([P, OUT], U32, align_bytes=64)
         w_scales = keep.tile([P, OUT], U8, align_bytes=64)
-        nc.vector.quantize_mx(out=w_codes[:].bitcast(FP8X4), scales=w_scales[:], in_=w_grouped[:])
-
-        nc.vector.tensor_copy(out=bias_square[0:1, :], in_=bias_row[:])
-        bias_flip = flip_psum.tile([P, N_TILE], F32, name="flip")
-        nc.tensor.transpose(bias_flip[:, 0:P], bias_square[:], ident[:])
+        w_grouped = keep.tile([P, OUT * PACK], BF16, align_bytes=64)
         bias_col = keep.tile([P, 1], F32)
-        nc.vector.tensor_copy(out=bias_col[:], in_=bias_flip[:, 0:1])
+
+        def prepare_weight_and_bias():
+            w_words = w_rows[:].bitcast(F32).rearrange("o (c hh) -> o hh c", hh=2)
+            flip = flip_psum.tile([P, N_TILE], F32, name="flip")
+            for hh in range(2):
+                nc.tensor.transpose(flip[:, hh * OUT : (hh + 1) * OUT], w_words[:, hh, :], ident[:])
+            nc.tensor.transpose(flip[:, 2 * OUT : 3 * OUT], bias_square[:], ident[:])
+            nc.vector.tensor_copy(
+                out=w_grouped[:].bitcast(F32).rearrange("c (o hh) -> c o hh", hh=2),
+                in_=flip[:, 0 : 2 * OUT].rearrange("c (hh o) -> c o hh", hh=2),
+            )
+            nc.vector.tensor_copy(out=bias_col[:], in_=flip[:, 2 * OUT : 2 * OUT + 1])
+
+        def quantise_weight():
+            nc.vector.quantize_mx(out=w_codes[:].bitcast(FP8X4), scales=w_scales[:], in_=w_grouped[:])
+
+
+        def term_to_planes(name, order, g, h, pool, tag, by_matmul, copy):
+            values = term_rows[name][:].rearrange("q (g s c b) -> q g s b c", g=CHUNKS, s=PACK, c=C)
+            flip = pool.tile([P, 2 * N_TILE], BF16, name=tag)
+            for eb in range(2):
+                for s in range(PACK):
+                    slot = eb * PACK + s
+                    out = flip[:, slot * P : (slot + 1) * P]
+                    in_ = values[:, g, s, 2 * h + eb, :]
+                    if by_matmul:
+                        nc.tensor.matmul(out, lhsT=in_, rhs=ident_half[:], start=True, stop=True)
+                    else:
+                        nc.tensor.transpose(out, in_, ident_half[:])
+            copy(out=planes[g][:, order, 2 * h : 2 * h + 2, :].rearrange("c eb v -> c (eb v)"), in_=flip[:])
 
         x2_codes = keep.tile([P, PASSES, CB], U32, align_bytes=64)
         x2_scales = keep.tile([P, PASSES, CB], U8, align_bytes=64)
         x2_grouped = {}
-        for g in range(PASSES + 1):
-            if g < PASSES:
-                grouped = two.tile([P, CB * PACK], BF16, align_bytes=64, name="x2_grouped")
-                nc.vector.tensor_copy(
-                    out=grouped[:].rearrange("q (b c t) -> q b c t", b=B, c=C),
-                    in_=term_rows["x2"][:, g * PACK * CB : (g + 1) * PACK * CB].rearrange(
-                        "q (t c b) -> q b c t", t=PACK, c=C
-                    ),
-                )
-                x2_grouped[g] = grouped
-            if g > 0:
-                nc.vector.quantize_mx(
-                    out=x2_codes[:, g - 1, :].bitcast(FP8X4), scales=x2_scales[:, g - 1, :], in_=x2_grouped[g - 1][:]
-                )
 
-        def transpose_term(name, order, g, h, copy):
-            words = term_rows[name][:].bitcast(F32).rearrange(
-                "q (g t c h) -> q g t h c", g=PASSES, t=PACK, c=C
+        def group_x2(g, h, copy):
+            words = planes[g][:].rearrange("c k b v -> c (k b v)").bitcast(F32).rearrange(
+                "c (k b uh q) -> c k b uh q", k=ORDERS, b=B, uh=2
             )
-            flip = flip_psum.tile([P, N_TILE], F32, name="flip")
-            for e in range(2):
-                for uh in range(2):
-                    slot = e * 2 + uh
-                    nc.tensor.transpose(flip[:, slot * P : (slot + 1) * P], words[:, g, 2 * uh + e, h, :], ident[:])
-            copy(
-                out=planes[g][:, order, 2 * h : 2 * h + 2, :].rearrange("c eb (n e) -> c eb n e", e=2),
-                in_=flip[:].bitcast(BF16).rearrange("c (e n eb) -> c eb n e", e=2, eb=2),
-            )
-
-        def transpose_x1(g, h, copy):
-            values = term_rows["x1"][:].rearrange("q (g s c b) -> q g s b c", g=PASSES, s=PACK, c=C)
-            flip = flip_psum.tile([P, 2 * N_TILE], BF16, name="flip")
+            grouped = four.tile([P, CB * PACK // 2], BF16, align_bytes=64, name="x2_grouped")
+            flip = acc_psum.tile([P, N_TILE], F32, name="acc")
             for eb in range(2):
-                for s in range(PACK):
-                    slot = eb * PACK + s
-                    nc.tensor.transpose(
-                        flip[:, slot * P : (slot + 1) * P], values[:, g, s, 2 * h + eb, :], ident_half[:]
-                    )
-            copy(out=planes[g][:, 1, 2 * h : 2 * h + 2, :].rearrange("c eb v -> c (eb v)"), in_=flip[:])
+                for uh in range(2):
+                    slot = eb * 2 + uh
+                    nc.tensor.transpose(flip[:, slot * P : (slot + 1) * P], words[:, 2, 2 * h + eb, uh, :], ident[:])
+            copy(
+                out=grouped[:].bitcast(F32).rearrange("q (eb c uh) -> q eb c uh", eb=2, c=C),
+                in_=flip[:].rearrange("q (eb uh c) -> q eb c uh", eb=2, uh=2),
+            )
+            x2_grouped[g, h] = grouped
 
-        for g in range(PASSES):
-            for h in range(2):
-                transpose_term("x2", 2, g, h, nc.scalar.copy)
+        def quantise_x2(g, h):
+            cols = slice(h * CB // 2, (h + 1) * CB // 2)
+            nc.vector.quantize_mx(
+                out=x2_codes[:, g, cols].bitcast(FP8X4), scales=x2_scales[:, g, cols], in_=x2_grouped[g, h][:]
+            )
 
         lap_grouped = {}
         lap_codes = {}
         lap_scales = {}
 
-        def transpose_lap_piece(piece, second_copy):
+        def transpose_lap_half(piece, a, copy):
             i, g = divmod(piece, PASSES)
-            words = lap_rows[i][:].bitcast(F32).rearrange("p (j w) -> p j w", j=PACK)
-            grouped = three.tile([P, N_TILE * PACK], BF16, align_bytes=64, name="lap_grouped")
-            grouped_words = grouped[:].bitcast(F32).rearrange("q (n uh) -> q n uh", uh=2)
-            for a in range(2):
-                flip = flip_psum.tile([P, N_TILE], F32, name="flip")
-                for jl in range(2):
-                    for uh in range(2):
-                        slot = jl * 2 + uh
-                        first = (K_PASS // 2) * g + P * uh
-                        nc.tensor.transpose(
-                            flip[:, slot * P : (slot + 1) * P], words[:, 2 * a + jl, first : first + P], ident[:]
-                        )
-                copy = (nc.scalar.copy, second_copy)[a]
-                copy(
-                    out=grouped_words[:, 2 * P * a : 2 * P * (a + 1), :].rearrange("q (jl p) uh -> q jl p uh", jl=2),
-                    in_=flip[:].rearrange("q (jl uh p) -> q jl p uh", jl=2, uh=2),
-                )
-            lap_grouped[piece] = grouped
+            words = lap_rows[i][:].rearrange("p j u -> p (j u)").bitcast(F32).rearrange("p (j w) -> p j w", j=PACK)
+            if a == 0:
+                lap_grouped[piece] = four.tile([P, N_TILE * PACK], BF16, align_bytes=64, name="lap_grouped")
+            grouped_words = lap_grouped[piece][:].bitcast(F32).rearrange("q (n uh) -> q n uh", uh=2)
+            flip = flip_psum.tile([P, N_TILE], F32, name="flip")
+            for jl in range(2):
+                for uh in range(2):
+                    slot = jl * 2 + uh
+                    first = (K_PASS // 2) * g + P * uh
+                    nc.tensor.transpose(
+                        flip[:, slot * P : (slot + 1) * P], words[:, 2 * a + jl, first : first + P], ident[:]
+                    )
+            copy(
+                out=grouped_words[:, 2 * P * a : 2 * P * (a + 1), :].rearrange("q (jl p) uh -> q jl p uh", jl=2),
+                in_=flip[:].rearrange("q (jl uh p) -> q jl p uh", jl=2, uh=2),
+            )
 
         def quantise_lap_piece(piece):
             i, g = divmod(piece, PASSES)
@@ -245,11 +237,12 @@ def tile_graph_conv_pb_kernel(tc, x0_dram, x1_dram, x2_dram, lap_dram, w_dram, b
                 in_=feat[unit][:].rearrange("c n k -> c (n k)"),
             )
 
+        y = {}
+
         def second_matmul(unit):
-            i, b = divmod(unit, B)
-            y = y_psum.tile([P, N_TILE], F32)
+            y[unit] = y_psum.tile([P, N_TILE], F32, name="y")
             nc.tensor.matmul_mx(
-                out=y[:],
+                out=y[unit][:],
                 lhsT=w_codes[:].bitcast(FP8X4),
                 lhsT_scale=w_scales[:],
                 rhs=feat_codes[unit][:].bitcast(FP8X4),
@@ -257,39 +250,70 @@ def tile_graph_conv_pb_kernel(tc, x0_dram, x1_dram, x2_dram, lap_dram, w_dram, b
                 start=True,
                 stop=True,
             )
-            y_sb = three.tile([P, N_TILE], F32)
-            nc.scalar.activation(
-                out=y_sb[:], in_=y[:], func=mybir.ActivationFunctionType.Identity, bias=bias_col[:, 0:1], scale=1.0
-            )
-            nc.scalar.dma_start(out=out_dram[b, :, i * N_TILE : (i + 1) * N_TILE], in_=y_sb[:])
 
-        for piece in range(PASSES + 1):
-            if piece < PASSES:
-                transpose_lap_piece(piece, nc.vector.tensor_copy)
+        def store(unit):
+            i, b = divmod(unit, B)
+            y_sb = four.tile([P, N_TILE], F32, name="y_sb")
+            nc.scalar.activation(
+                out=y_sb[:], in_=y[unit][:], func=mybir.ActivationFunctionType.Identity, bias=bias_col[:, 0:1], scale=1.0
+            )
+            nc.sync.dma_start(out=out_dram[b, :, i * N_TILE : (i + 1) * N_TILE], in_=y_sb[:])
+
+        v_copy = nc.vector.tensor_copy
+        s_copy = nc.scalar.copy
+
+        def transpose_lap_piece(piece, copies):
+            for a in range(2):
+                transpose_lap_half(piece, a, copies[a])
+
+        halves = [(g, h) for g in range(PASSES) for h in range(2)]
+        for n in range(len(halves) + 3):
+            if n < len(halves):
+                term_to_planes("x2", 2, *halves[n], flip_psum, "flip", True, s_copy)
+            if 2 <= n < len(halves) + 2:
+                group_x2(*halves[n - 2], (s_copy if n % 3 == 2 else v_copy))
+            if n >= 3:
+                quantise_x2(*halves[n - 3])
+        for piece in range(PASSES):
+            transpose_lap_piece(piece, (s_copy, v_copy))
             if piece > 0:
                 quantise_lap_piece(piece - 1)
-        transposed = PASSES
-        transpose_x1(0, 0, nc.scalar.copy)
-        transpose_x1(0, 1, nc.vector.tensor_copy)
-
+        for h in range(2):
+            term_to_planes("x1", 1, 0, h, y_psum, "y", True, s_copy)
+        quantise_lap_piece(PASSES - 1)
+        nc.vector.tensor_copy(out=bias_square[0:1, :], in_=bias_row[:])
         first_matmul(0)
+        first_matmul(1)
+        for piece in range(PASSES, PASSES + 2):
+            transpose_lap_piece(piece, (s_copy, s_copy))
+        transposed = PASSES + 2
+        quantised = PASSES
+
+
         for unit in range(UNITS + 1):
             i, b = divmod(unit, B)
+            split = N_TILE - (SCALAR_COLS if unit + PASSES < LAP_PASSES else SCALAR_COLS_END)
             if unit < UNITS:
                 third_term(unit)
-                feat[unit] = three.tile([P, N_TILE, ORDERS], BF16, align_bytes=64, name="feat")
-                interleave_features(unit, nc.scalar.copy, slice(N_TILE - SCALAR_COLS, N_TILE))
-            while transposed < min(unit + LEAD + 1, LAP_PASSES):
-                transpose_lap_piece(transposed, nc.scalar.copy)
-                transposed += 1
-            if i + 1 < CHUNKS and b % 2 == 0:
-                transpose_x1(i + 1, b // 2, nc.scalar.copy)
-            if unit + PASSES < LAP_PASSES:
-                quantise_lap_piece(unit + PASSES)
-            if unit + 1 < UNITS:
+            if 0 < unit < UNITS - 1:
                 first_matmul(unit + 1)
             if unit > 0:
                 quantise_features(unit - 1)
                 second_matmul(unit - 1)
             if unit < UNITS:
-                interleave_features(unit, nc.vector.tensor_copy, slice(0, N_TILE - SCALAR_COLS))
+                feat[unit] = three.tile([P, N_TILE, ORDERS], BF16, align_bytes=64, name="feat")
+                interleave_features(unit, s_copy, slice(split, N_TILE))
+                interleave_features(unit, v_copy, slice(0, split))
+            if unit == 0:
+                prepare_weight_and_bias()
+                quantise_weight()
+            for piece in range(transposed, min(unit + LEAD + 1, LAP_PASSES)):
+                transpose_lap_piece(piece, (s_copy, s_copy))
+                transposed += 1
+            if i + 1 < CHUNKS and b % 2 == 0:
+                term_to_planes("x1", 1, i + 1, b // 2, flip_psum, "flip", False, s_copy)
+            if unit > 0:
+                store(unit - 1)
+            for piece in range(quantised, min(unit + LEAD, LAP_PASSES)):
+                quantise_lap_piece(piece)
+                quantised += 1

@@ -20,9 +20,9 @@ CHUNKS = V // N_TILE
 PASSES = V // K_PASS
 UNITS = CHUNKS * B
 LAP_PASSES = CHUNKS * PASSES
-LEAD = 6
+LEAD = 5
 SCALAR_COLS = 128
-SCALAR_COLS_END = 192
+SCALAR_COLS_END = 256
 
 FLOPS = 2 * V * V * CB + 2 * B * V * C * ORDERS * OUT
 
@@ -55,14 +55,16 @@ def tile_graph_conv_pb_kernel(tc, x0_dram, x1_dram, x2_dram, lap_dram, w_dram, b
         }
         term_views = {
             "x1": x1_dram.rearrange("(g s q) w -> g q s w", g=CHUNKS, s=PACK, q=P),
-            "x2": x2_dram.rearrange("(g s q) w -> g q s w", g=CHUNKS, s=PACK, q=P),
+            "x2": x2_dram.rearrange("(g uh q e) w -> g q uh (e w)", g=CHUNKS, uh=2, q=P, e=2),
         }
 
-        def load_term_chunk(name, g, slots=slice(0, PACK)):
-            rows = term_rows[name][:, g * PACK * CB : (g + 1) * PACK * CB].rearrange("q (s w) -> q s w", s=PACK)
-            nc.sync.dma_start(out=rows[:, slots, :], in_=term_views[name][g][:, slots, :])
+        def load_term_chunk(name, g):
+            rows = term_rows[name][:, g * PACK * CB : (g + 1) * PACK * CB]
+            nc.sync.dma_start(
+                out=rows.rearrange("q (r w) -> q r w", r=term_views[name].shape[2]), in_=term_views[name][g]
+            )
 
-        lap_view = lap_dram.rearrange("(i p j) u -> i p j u", i=CHUNKS, p=P, j=PACK)
+        lap_view = lap_dram.rearrange("(i j p) u -> i p j u", i=CHUNKS, p=P, j=PACK)
         lap_rows = {}
 
         def load_lap_half(i, a):
@@ -82,81 +84,98 @@ def tile_graph_conv_pb_kernel(tc, x0_dram, x1_dram, x2_dram, lap_dram, w_dram, b
 
         w_rows = keep.tile([OUT, C * ORDERS], BF16)
         bias_row = keep.tile([1, OUT], BF16)
-        load_term_chunk("x2", 0, slice(0, 2))
-        load_term_chunk("x2", 0, slice(2, PACK))
-        for g in range(1, PASSES):
+        for g in range(PASSES):
             load_term_chunk("x2", g)
         load_lap_half(0, 0)
-        load_lap_half(0, 1)
-        load_term_chunk("x1", 0)
         nc.sync.dma_start(out=bias_row[:], in_=bias_dram.rearrange("(one o) -> one o", one=1))
         nc.sync.dma_start(out=w_rows[:], in_=w_dram)
+        load_lap_half(0, 1)
+        load_term_chunk("x1", 0)
         load_x0_chunk(0)
-        for i in range(1, CHUNKS):
-            load_lap_half(i, 0)
-            load_lap_half(i, 1)
-            load_term_chunk("x1", i)
-            load_x0_chunk(i)
 
         w_codes = keep.tile([P, OUT], U32, align_bytes=64)
         w_scales = keep.tile([P, OUT], U8, align_bytes=64)
         w_grouped = keep.tile([P, OUT * PACK], BF16, align_bytes=64)
         bias_col = keep.tile([P, 1], F32)
 
-        def prepare_weight_and_bias():
+        w_flip = {}
+
+        def transpose_weight_and_bias():
             w_words = w_rows[:].bitcast(F32).rearrange("o (c hh) -> o hh c", hh=2)
             flip = flip_psum.tile([P, N_TILE], F32, name="flip")
             for hh in range(2):
                 nc.tensor.transpose(flip[:, hh * OUT : (hh + 1) * OUT], w_words[:, hh, :], ident[:])
             nc.tensor.transpose(flip[:, 2 * OUT : 3 * OUT], bias_square[:], ident[:])
+            w_flip[0] = flip
+
+        def copy_weight_and_bias():
+            flip = w_flip[0]
             nc.vector.tensor_copy(
                 out=w_grouped[:].bitcast(F32).rearrange("c (o hh) -> c o hh", hh=2),
                 in_=flip[:, 0 : 2 * OUT].rearrange("c (hh o) -> c o hh", hh=2),
             )
             nc.vector.tensor_copy(out=bias_col[:], in_=flip[:, 2 * OUT : 2 * OUT + 1])
 
+        def prepare_weight_and_bias():
+            transpose_weight_and_bias()
+            copy_weight_and_bias()
+
         def quantise_weight():
             nc.vector.quantize_mx(out=w_codes[:].bitcast(FP8X4), scales=w_scales[:], in_=w_grouped[:])
 
 
+        x2_late = {}
+
+        def load_x2_late(g):
+            x2_late[g] = two.tile([P, CB * PACK], BF16, align_bytes=64, name="x2_grouped")
+            nc.sync.dma_start(
+                out=x2_late[g][:].rearrange("q (s w) -> q s w", s=PACK),
+                in_=x2_dram.rearrange("(g s q) w -> g q s w", g=CHUNKS, s=PACK, q=P)[g],
+            )
+
         def term_to_planes(name, order, g, h, pool, tag, by_matmul, copy):
-            values = term_rows[name][:].rearrange("q (g s c b) -> q g s b c", g=CHUNKS, s=PACK, c=C)
+            rows = x2_late[g][:] if order == 2 else term_rows[name][:, g * PACK * CB : (g + 1) * PACK * CB]
+            values = rows.rearrange("q (s c b) -> q s b c", s=PACK, c=C)
             flip = pool.tile([P, 2 * N_TILE], BF16, name=tag)
             for eb in range(2):
                 for s in range(PACK):
                     slot = eb * PACK + s
                     out = flip[:, slot * P : (slot + 1) * P]
-                    in_ = values[:, g, s, 2 * h + eb, :]
+                    in_ = values[:, s, 2 * h + eb, :]
                     if by_matmul:
                         nc.tensor.matmul(out, lhsT=in_, rhs=ident_half[:], start=True, stop=True)
                     else:
                         nc.tensor.transpose(out, in_, ident_half[:])
             copy(out=planes[g][:, order, 2 * h : 2 * h + 2, :].rearrange("c eb v -> c (eb v)"), in_=flip[:])
 
+        def x2_pairs_to_planes(g, h, copy):
+            words = term_rows["x2"][:].bitcast(F32).rearrange("q (g t c h) -> q g t h c", g=PASSES, t=PACK, c=C)
+            flip = flip_psum.tile([P, N_TILE], F32, name="flip")
+            for e in range(2):
+                for uh in range(2):
+                    slot = e * 2 + uh
+                    nc.tensor.transpose(flip[:, slot * P : (slot + 1) * P], words[:, g, 2 * uh + e, h, :], ident[:])
+            copy(
+                out=planes[g][:, 2, 2 * h : 2 * h + 2, :].rearrange("c eb (n e) -> c eb n e", e=2),
+                in_=flip[:].bitcast(BF16).rearrange("c (e n eb) -> c eb n e", e=2, eb=2),
+            )
+
         x2_codes = keep.tile([P, PASSES, CB], U32, align_bytes=64)
         x2_scales = keep.tile([P, PASSES, CB], U8, align_bytes=64)
         x2_grouped = {}
 
-        def group_x2(g, h, copy):
-            words = planes[g][:].rearrange("c k b v -> c (k b v)").bitcast(F32).rearrange(
-                "c (k b uh q) -> c k b uh q", k=ORDERS, b=B, uh=2
+        def group_x2(g):
+            x2_grouped[g] = two.tile([P, CB * PACK], BF16, align_bytes=64, name="x2_grouped")
+            nc.vector.tensor_copy(
+                out=x2_grouped[g][:].rearrange("q (b c t) -> q b c t", b=B, c=C),
+                in_=term_rows["x2"][:, g * PACK * CB : (g + 1) * PACK * CB].rearrange(
+                    "q (t c b) -> q b c t", t=PACK, c=C
+                ),
             )
-            grouped = four.tile([P, CB * PACK // 2], BF16, align_bytes=64, name="x2_grouped")
-            flip = acc_psum.tile([P, N_TILE], F32, name="acc")
-            for eb in range(2):
-                for uh in range(2):
-                    slot = eb * 2 + uh
-                    nc.tensor.transpose(flip[:, slot * P : (slot + 1) * P], words[:, 2, 2 * h + eb, uh, :], ident[:])
-            copy(
-                out=grouped[:].bitcast(F32).rearrange("q (eb c uh) -> q eb c uh", eb=2, c=C),
-                in_=flip[:].rearrange("q (eb uh c) -> q eb c uh", eb=2, uh=2),
-            )
-            x2_grouped[g, h] = grouped
 
-        def quantise_x2(g, h):
-            cols = slice(h * CB // 2, (h + 1) * CB // 2)
+        def quantise_x2(g):
             nc.vector.quantize_mx(
-                out=x2_codes[:, g, cols].bitcast(FP8X4), scales=x2_scales[:, g, cols], in_=x2_grouped[g, h][:]
+                out=x2_codes[:, g, :].bitcast(FP8X4), scales=x2_scales[:, g, :], in_=x2_grouped[g][:]
             )
 
         lap_grouped = {}
@@ -213,10 +232,10 @@ def tile_graph_conv_pb_kernel(tc, x0_dram, x1_dram, x2_dram, lap_dram, w_dram, b
         def third_term(unit):
             i, b = divmod(unit, B)
             nc.vector.scalar_tensor_tensor(
-                out=planes[i][:, 3, b, :].rearrange("c (p j) -> c p j", j=PACK),
-                in0=acc[unit][:].rearrange("c (j p) -> c p j", j=PACK),
+                out=planes[i][:, 3, b, :],
+                in0=acc[unit][:],
                 scalar=2.0,
-                in1=planes[i][:, 1, b, :].rearrange("c (p j) -> c p j", j=PACK),
+                in1=planes[i][:, 1, b, :],
                 op0=mult,
                 op1=subtract,
             )
@@ -228,36 +247,45 @@ def tile_graph_conv_pb_kernel(tc, x0_dram, x1_dram, x2_dram, lap_dram, w_dram, b
                 in_=planes[i][:, :, b, cols].rearrange("c k (n r) -> c n k r", r=4),
             )
 
-        def quantise_features(unit):
-            feat_codes[unit] = three.tile([P, N_TILE], U32, align_bytes=64, name="feat_codes")
-            feat_scales[unit] = three.tile([P, N_TILE], U8, align_bytes=64, name="feat_scales")
+        def quantise_features(unit, cols=slice(0, N_TILE)):
+            if cols.start == 0:
+                feat_codes[unit] = three.tile([P, N_TILE], U32, align_bytes=64, name="feat_codes")
+                feat_scales[unit] = three.tile([P, N_TILE], U8, align_bytes=64, name="feat_scales")
             nc.vector.quantize_mx(
-                out=feat_codes[unit][:].bitcast(FP8X4),
-                scales=feat_scales[unit][:],
-                in_=feat[unit][:].rearrange("c n k -> c (n k)"),
+                out=feat_codes[unit][:, cols].bitcast(FP8X4),
+                scales=feat_scales[unit][:, cols],
+                in_=feat[unit][:, cols, :].rearrange("c n k -> c (n k)"),
             )
 
-        y = {}
-
-        def second_matmul(unit):
-            y[unit] = y_psum.tile([P, N_TILE], F32, name="y")
+        def second_matmul(unit, cols=slice(0, N_TILE)):
+            y = y_psum.tile([P, N_TILE], F32, name="y")
             nc.tensor.matmul_mx(
-                out=y[unit][:],
+                out=y[:, cols],
                 lhsT=w_codes[:].bitcast(FP8X4),
                 lhsT_scale=w_scales[:],
-                rhs=feat_codes[unit][:].bitcast(FP8X4),
-                rhs_scale=feat_scales[unit][:],
+                rhs=feat_codes[unit][:, cols].bitcast(FP8X4),
+                rhs_scale=feat_scales[unit][:, cols],
                 start=True,
                 stop=True,
             )
+            return y
 
-        def store(unit):
-            i, b = divmod(unit, B)
-            y_sb = four.tile([P, N_TILE], F32, name="y_sb")
+        def add_bias_on_scalar(out, y):
             nc.scalar.activation(
-                out=y_sb[:], in_=y[unit][:], func=mybir.ActivationFunctionType.Identity, bias=bias_col[:, 0:1], scale=1.0
+                out=out, in_=y, func=mybir.ActivationFunctionType.Identity, bias=bias_col[:, 0:1], scale=1.0
             )
-            nc.sync.dma_start(out=out_dram[b, :, i * N_TILE : (i + 1) * N_TILE], in_=y_sb[:])
+
+        def add_bias_on_vector(out, y):
+            nc.vector.tensor_scalar(out=out, in0=y, scalar1=bias_col[:, 0:1], scalar2=None, op0=mybir.AluOpType.add)
+
+        def store(unit, y, add_bias=add_bias_on_scalar, cols=slice(0, N_TILE)):
+            i, b = divmod(unit, B)
+            width = cols.stop - cols.start
+            y_sb = four.tile([P, width], F32, name="y_sb%d" % width)
+            add_bias(y_sb[:], y[:, cols])
+            nc.sync.dma_start(
+                out=out_dram[b, :, i * N_TILE + cols.start : i * N_TILE + cols.stop], in_=y_sb[:]
+            )
 
         v_copy = nc.vector.tensor_copy
         s_copy = nc.scalar.copy
@@ -266,54 +294,80 @@ def tile_graph_conv_pb_kernel(tc, x0_dram, x1_dram, x2_dram, lap_dram, w_dram, b
             for a in range(2):
                 transpose_lap_half(piece, a, copies[a])
 
-        halves = [(g, h) for g in range(PASSES) for h in range(2)]
-        for n in range(len(halves) + 3):
-            if n < len(halves):
-                term_to_planes("x2", 2, *halves[n], flip_psum, "flip", True, s_copy)
-            if 2 <= n < len(halves) + 2:
-                group_x2(*halves[n - 2], (s_copy if n % 3 == 2 else v_copy))
-            if n >= 3:
-                quantise_x2(*halves[n - 3])
+        for g in range(PASSES + 1):
+            if g < PASSES:
+                group_x2(g)
+                if g < 3:
+                    for h in range(2):
+                        x2_pairs_to_planes(g, h, s_copy)
+            if g > 0:
+                quantise_x2(g - 1)
+
+        for i in range(1, CHUNKS):
+            load_lap_half(i, 0)
+            load_lap_half(i, 1)
+            load_term_chunk("x1", i)
+            load_x0_chunk(i)
+            if i + 2 < CHUNKS:
+                load_x2_late(i + 2)
+
+        nc.vector.tensor_copy(out=bias_square[0:1, :], in_=bias_row[:])
         for piece in range(PASSES):
-            transpose_lap_piece(piece, (s_copy, v_copy))
+            if piece == 2:
+                prepare_weight_and_bias()
+                quantise_weight()
+            transpose_lap_piece(piece, (s_copy, (s_copy, v_copy)[piece % 2]))
             if piece > 0:
                 quantise_lap_piece(piece - 1)
-        for h in range(2):
-            term_to_planes("x1", 1, 0, h, y_psum, "y", True, s_copy)
         quantise_lap_piece(PASSES - 1)
-        nc.vector.tensor_copy(out=bias_square[0:1, :], in_=bias_row[:])
+        term_to_planes("x1", 1, 0, 0, y_psum, "y", True, s_copy)
         first_matmul(0)
+        term_to_planes("x1", 1, 0, 1, y_psum, "y", True, s_copy)
         first_matmul(1)
-        for piece in range(PASSES, PASSES + 2):
-            transpose_lap_piece(piece, (s_copy, s_copy))
-        transposed = PASSES + 2
+        transpose_lap_piece(PASSES, (s_copy, s_copy))
+        transposed = PASSES + 1
         quantised = PASSES
 
 
-        for unit in range(UNITS + 1):
+        y = {}
+        for unit in range(UNITS - 1):
             i, b = divmod(unit, B)
-            split = N_TILE - (SCALAR_COLS if unit + PASSES < LAP_PASSES else SCALAR_COLS_END)
-            if unit < UNITS:
-                third_term(unit)
-            if 0 < unit < UNITS - 1:
-                first_matmul(unit + 1)
+            third_term(unit)
+            for piece in range(quantised, min(unit + LEAD, LAP_PASSES) if unit > 0 else quantised):
+                quantise_lap_piece(piece)
+                quantised += 1
             if unit > 0:
                 quantise_features(unit - 1)
-                second_matmul(unit - 1)
-            if unit < UNITS:
-                feat[unit] = three.tile([P, N_TILE, ORDERS], BF16, align_bytes=64, name="feat")
-                interleave_features(unit, s_copy, slice(split, N_TILE))
-                interleave_features(unit, v_copy, slice(0, split))
-            if unit == 0:
-                prepare_weight_and_bias()
-                quantise_weight()
             for piece in range(transposed, min(unit + LEAD + 1, LAP_PASSES)):
                 transpose_lap_piece(piece, (s_copy, s_copy))
                 transposed += 1
-            if i + 1 < CHUNKS and b % 2 == 0:
-                term_to_planes("x1", 1, i + 1, b // 2, flip_psum, "flip", False, s_copy)
-            if unit > 0:
-                store(unit - 1)
-            for piece in range(quantised, min(unit + LEAD, LAP_PASSES)):
-                quantise_lap_piece(piece)
-                quantised += 1
+            feat[unit] = three.tile([P, N_TILE, ORDERS], BF16, align_bytes=64, name="feat")
+            split = N_TILE - (64 if unit < 4 else SCALAR_COLS if unit + PASSES < LAP_PASSES else SCALAR_COLS_END)
+            interleave_features(unit, s_copy, slice(split, N_TILE))
+            if i + 1 < CHUNKS and b >= 2:
+                term_to_planes("x1", 1, i + 1, b - 2, flip_psum, "flip", False, s_copy)
+            if i == 1 and b < 2:
+                term_to_planes("x2", 2, i + 2, b, flip_psum, "flip", True, s_copy)
+            if 0 < unit < UNITS - 1:
+                first_matmul(unit + 1)
+            if unit >= 2:
+                y[unit - 2] = second_matmul(unit - 2)
+            if unit >= 2:
+                store(unit - 2, y[unit - 2])
+            interleave_features(unit, v_copy, slice(0, split))
+
+        last = UNITS - 1
+        half = N_TILE // 2
+        third_term(last)
+        quantise_features(last - 1)
+        y[last - 2] = second_matmul(last - 2)
+        feat[last] = three.tile([P, N_TILE, ORDERS], BF16, align_bytes=64, name="feat")
+        interleave_features(last, s_copy, slice(N_TILE - 128, N_TILE))
+        store(last - 2, y[last - 2])
+        interleave_features(last, v_copy, slice(0, half))
+        interleave_features(last, v_copy, slice(half, N_TILE - 128))
+        y[last - 1] = second_matmul(last - 1)
+        store(last - 1, y[last - 1])
+        for cols, add_bias in ((slice(0, half), add_bias_on_scalar), (slice(half, N_TILE), add_bias_on_vector)):
+            quantise_features(last, cols)
+            store(last, second_matmul(last, cols), add_bias, cols)

@@ -35,6 +35,7 @@ def tile_graph_conv_pb_kernel(tc, x0_dram, x1_dram, x2_dram, lap_dram, w_dram, b
     with ExitStack() as ctx:
         keep = ctx.enter_context(tc.tile_pool(name="keep", bufs=1))
         two = ctx.enter_context(tc.tile_pool(name="two", bufs=2))
+        eight = ctx.enter_context(tc.tile_pool(name="eight", bufs=8))
         four = ctx.enter_context(tc.tile_pool(name="four", bufs=4))
         three = ctx.enter_context(tc.tile_pool(name="three", bufs=3))
         flip_psum = ctx.enter_context(tc.psum_pool(name="flip", bufs=4))
@@ -49,29 +50,38 @@ def tile_graph_conv_pb_kernel(tc, x0_dram, x1_dram, x2_dram, lap_dram, w_dram, b
         bias_square = keep.tile([P, P], F32)
         nc.vector.memset(bias_square[:], 0.0)
 
-        term_rows = {
-            "x1": keep.tile([P, CHUNKS * PACK * CB], BF16, name="x1_rows"),
-            "x2": keep.tile([P, CHUNKS * PACK * CB], BF16, name="x2_rows"),
-        }
+        term_rows = {"x2": keep.tile([P, CHUNKS * PACK * CB], BF16, name="x2_rows")}
+        x1_rows = {}
         term_views = {
             "x1": x1_dram.rearrange("(g s q) w -> g q s w", g=CHUNKS, s=PACK, q=P),
             "x2": x2_dram.rearrange("(g uh q e) w -> g q uh (e w)", g=CHUNKS, uh=2, q=P, e=2),
         }
 
         def load_term_chunk(name, g):
-            rows = term_rows[name][:, g * PACK * CB : (g + 1) * PACK * CB]
+            if name == "x1":
+                x1_rows[g] = two.tile([P, PACK * CB], BF16, name="x1_rows")
+                rows = x1_rows[g][:]
+            else:
+                rows = term_rows[name][:, g * PACK * CB : (g + 1) * PACK * CB]
             nc.sync.dma_start(
                 out=rows.rearrange("q (r w) -> q r w", r=term_views[name].shape[2]), in_=term_views[name][g]
             )
 
-        lap_view = lap_dram.rearrange("(i j p) u -> i p j u", i=CHUNKS, p=P, j=PACK)
+        lap_view = lap_dram.rearrange("(i p j) u -> i p j u", i=CHUNKS, p=P, j=PACK)
         lap_rows = {}
 
         def load_lap_half(i, a):
             if a == 0:
                 lap_rows[i] = three.tile([P, PACK, V], BF16, name="lap_rows")
-            half = slice(a * V // 2, (a + 1) * V // 2)
-            nc.sync.dma_start(out=lap_rows[i][:, :, half], in_=lap_view[i][:, :, half])
+            if i == 0:
+                half = slice(a * V // 2, (a + 1) * V // 2)
+                nc.sync.dma_start(out=lap_rows[i][:, :, half], in_=lap_view[i][:, :, half])
+            else:
+                half = slice(a * PACK // 2, (a + 1) * PACK // 2)
+                nc.sync.dma_start(
+                    out=lap_rows[i][:, half, :].rearrange("p j u -> p (j u)"),
+                    in_=lap_view[i][:, half, :].rearrange("p j u -> p (j u)"),
+                )
 
         x0_view = x0_dram.rearrange("b c v -> c b v")
         planes = {}
@@ -124,17 +134,8 @@ def tile_graph_conv_pb_kernel(tc, x0_dram, x1_dram, x2_dram, lap_dram, w_dram, b
             nc.vector.quantize_mx(out=w_codes[:].bitcast(FP8X4), scales=w_scales[:], in_=w_grouped[:])
 
 
-        x2_late = {}
-
-        def load_x2_late(g):
-            x2_late[g] = two.tile([P, CB * PACK], BF16, align_bytes=64, name="x2_grouped")
-            nc.sync.dma_start(
-                out=x2_late[g][:].rearrange("q (s w) -> q s w", s=PACK),
-                in_=x2_dram.rearrange("(g s q) w -> g q s w", g=CHUNKS, s=PACK, q=P)[g],
-            )
-
         def term_to_planes(name, order, g, h, pool, tag, by_matmul, copy):
-            rows = x2_late[g][:] if order == 2 else term_rows[name][:, g * PACK * CB : (g + 1) * PACK * CB]
+            rows = x1_rows[g][:]
             values = rows.rearrange("q (s c b) -> q s b c", s=PACK, c=C)
             flip = pool.tile([P, 2 * N_TILE], BF16, name=tag)
             for eb in range(2):
@@ -232,10 +233,10 @@ def tile_graph_conv_pb_kernel(tc, x0_dram, x1_dram, x2_dram, lap_dram, w_dram, b
         def third_term(unit):
             i, b = divmod(unit, B)
             nc.vector.scalar_tensor_tensor(
-                out=planes[i][:, 3, b, :],
-                in0=acc[unit][:],
+                out=planes[i][:, 3, b, :].rearrange("c (p j) -> c p j", j=PACK),
+                in0=acc[unit][:].rearrange("c (j p) -> c p j", j=PACK),
                 scalar=2.0,
-                in1=planes[i][:, 1, b, :],
+                in1=planes[i][:, 1, b, :].rearrange("c (p j) -> c p j", j=PACK),
                 op0=mult,
                 op1=subtract,
             )
@@ -281,7 +282,7 @@ def tile_graph_conv_pb_kernel(tc, x0_dram, x1_dram, x2_dram, lap_dram, w_dram, b
         def store(unit, y, add_bias=add_bias_on_scalar, cols=slice(0, N_TILE)):
             i, b = divmod(unit, B)
             width = cols.stop - cols.start
-            y_sb = four.tile([P, width], F32, name="y_sb%d" % width)
+            y_sb = eight.tile([P, width], F32, name="y_sb%d" % width)
             add_bias(y_sb[:], y[:, cols])
             nc.sync.dma_start(
                 out=out_dram[b, :, i * N_TILE + cols.start : i * N_TILE + cols.stop], in_=y_sb[:]
@@ -308,8 +309,6 @@ def tile_graph_conv_pb_kernel(tc, x0_dram, x1_dram, x2_dram, lap_dram, w_dram, b
             load_lap_half(i, 1)
             load_term_chunk("x1", i)
             load_x0_chunk(i)
-            if i + 2 < CHUNKS:
-                load_x2_late(i + 2)
 
         nc.vector.tensor_copy(out=bias_square[0:1, :], in_=bias_row[:])
         for piece in range(PASSES):
@@ -332,8 +331,10 @@ def tile_graph_conv_pb_kernel(tc, x0_dram, x1_dram, x2_dram, lap_dram, w_dram, b
         y = {}
         for unit in range(UNITS - 1):
             i, b = divmod(unit, B)
+            feat[unit] = three.tile([P, N_TILE, ORDERS], BF16, align_bytes=64, name="feat")
+            split = N_TILE - (64 if unit < 4 else SCALAR_COLS if unit + PASSES < LAP_PASSES else SCALAR_COLS_END)
             third_term(unit)
-            for piece in range(quantised, min(unit + LEAD, LAP_PASSES) if unit > 0 else quantised):
+            for piece in range(quantised, min(unit + LEAD if unit > 0 else quantised, LAP_PASSES)):
                 quantise_lap_piece(piece)
                 quantised += 1
             if unit > 0:
@@ -341,13 +342,11 @@ def tile_graph_conv_pb_kernel(tc, x0_dram, x1_dram, x2_dram, lap_dram, w_dram, b
             for piece in range(transposed, min(unit + LEAD + 1, LAP_PASSES)):
                 transpose_lap_piece(piece, (s_copy, s_copy))
                 transposed += 1
-            feat[unit] = three.tile([P, N_TILE, ORDERS], BF16, align_bytes=64, name="feat")
-            split = N_TILE - (64 if unit < 4 else SCALAR_COLS if unit + PASSES < LAP_PASSES else SCALAR_COLS_END)
             interleave_features(unit, s_copy, slice(split, N_TILE))
             if i + 1 < CHUNKS and b >= 2:
                 term_to_planes("x1", 1, i + 1, b - 2, flip_psum, "flip", False, s_copy)
             if i == 1 and b < 2:
-                term_to_planes("x2", 2, i + 2, b, flip_psum, "flip", True, s_copy)
+                x2_pairs_to_planes(PASSES - 1, b, s_copy)
             if 0 < unit < UNITS - 1:
                 first_matmul(unit + 1)
             if unit >= 2:

@@ -244,8 +244,8 @@ def tile_graph_conv_pb_kernel(tc, x0_dram, x1_dram, x2_dram, lap_dram, w_dram, b
         def interleave_features(unit, copy, cols):
             i, b = divmod(unit, B)
             copy(
-                out=feat[unit][:, cols, :].rearrange("c (n r) k -> c n k r", r=4),
-                in_=planes[i][:, :, b, cols].rearrange("c k (n r) -> c n k r", r=4),
+                out=feat[unit][:, cols, :].rearrange("c (n r) k -> c n k r", r=8),
+                in_=planes[i][:, :, b, cols].rearrange("c k (n r) -> c n k r", r=8),
             )
 
         def quantise_features(unit, cols=slice(0, N_TILE)):

@@ -149,18 +149,6 @@ def tile_graph_conv_pb_kernel(tc, x0_dram, x1_dram, x2_dram, lap_dram, w_dram, b
                         nc.tensor.transpose(out, in_, ident_half[:])
             copy(out=planes[g][:, order, 2 * h : 2 * h + 2, :].rearrange("c eb v -> c (eb v)"), in_=flip[:])
 
-        def x2_pairs_to_planes(g, h, copy):
-            words = term_rows["x2"][:].bitcast(F32).rearrange("q (g t c h) -> q g t h c", g=PASSES, t=PACK, c=C)
-            flip = flip_psum.tile([P, N_TILE], F32, name="flip")
-            for e in range(2):
-                for uh in range(2):
-                    slot = e * 2 + uh
-                    nc.tensor.transpose(flip[:, slot * P : (slot + 1) * P], words[:, g, 2 * uh + e, h, :], ident[:])
-            copy(
-                out=planes[g][:, 2, 2 * h : 2 * h + 2, :].rearrange("c eb (n e) -> c eb n e", e=2),
-                in_=flip[:].bitcast(BF16).rearrange("c (e n eb) -> c eb n e", e=2, eb=2),
-            )
-
         x2_codes = keep.tile([P, PASSES, CB], U32, align_bytes=64)
         x2_scales = keep.tile([P, PASSES, CB], U8, align_bytes=64)
         x2_grouped = {}
@@ -172,6 +160,17 @@ def tile_graph_conv_pb_kernel(tc, x0_dram, x1_dram, x2_dram, lap_dram, w_dram, b
                 in_=term_rows["x2"][:, g * PACK * CB : (g + 1) * PACK * CB].rearrange(
                     "q (t c b) -> q b c t", t=PACK, c=C
                 ),
+            )
+
+        def x2_to_planes(g, h):
+            words = x2_grouped[g][:].bitcast(F32).rearrange("q (b c uh) -> q b uh c", b=B, c=C)
+            flip = flip_psum.tile([P, N_TILE], F32, name="flip")
+            for eb in range(2):
+                for uh in range(2):
+                    slot = eb * 2 + uh
+                    nc.tensor.transpose(flip[:, slot * P : (slot + 1) * P], words[:, 2 * h + eb, uh, :], ident[:])
+            nc.scalar.copy(
+                out=planes[g][:, 2, 2 * h : 2 * h + 2, :].rearrange("c eb v -> c (eb v)").bitcast(F32), in_=flip[:]
             )
 
         def quantise_x2(g):
@@ -300,7 +299,7 @@ def tile_graph_conv_pb_kernel(tc, x0_dram, x1_dram, x2_dram, lap_dram, w_dram, b
                 group_x2(g)
                 if g < 3:
                     for h in range(2):
-                        x2_pairs_to_planes(g, h, s_copy)
+                        x2_to_planes(g, h)
             if g > 0:
                 quantise_x2(g - 1)
 
@@ -346,7 +345,7 @@ def tile_graph_conv_pb_kernel(tc, x0_dram, x1_dram, x2_dram, lap_dram, w_dram, b
             if i + 1 < CHUNKS and b >= 2:
                 term_to_planes("x1", 1, i + 1, b - 2, flip_psum, "flip", False, s_copy)
             if i == 1 and b < 2:
-                x2_pairs_to_planes(PASSES - 1, b, s_copy)
+                x2_to_planes(PASSES - 1, b)
             if 0 < unit < UNITS - 1:
                 first_matmul(unit + 1)
             if unit >= 2:

@@ -21,7 +21,7 @@ PASSES = V // K_PASS
 UNITS = CHUNKS * B
 LAP_PASSES = CHUNKS * PASSES
 LEAD = 5
-SCALAR_COLS = 128
+SCALAR_COLS = 144
 SCALAR_COLS_END = 256
 
 FLOPS = 2 * V * V * CB + 2 * B * V * C * ORDERS * OUT
@@ -147,7 +147,10 @@ def tile_graph_conv_pb_kernel(tc, x0_dram, x1_dram, x2_dram, lap_dram, w_dram, b
                         nc.tensor.matmul(out, lhsT=in_, rhs=ident_half[:], start=True, stop=True)
                     else:
                         nc.tensor.transpose(out, in_, ident_half[:])
-            copy(out=planes[g][:, order, 2 * h : 2 * h + 2, :].rearrange("c eb v -> c (eb v)"), in_=flip[:])
+            copy(
+                out=planes[g][:, order, 2 * h : 2 * h + 2, :].rearrange("c eb v -> c (eb v)").bitcast(F32),
+                in_=flip[:].bitcast(F32),
+            )
 
         x2_codes = keep.tile([P, PASSES, CB], U32, align_bytes=64)
         x2_scales = keep.tile([P, PASSES, CB], U8, align_bytes=64)
@@ -331,7 +334,7 @@ def tile_graph_conv_pb_kernel(tc, x0_dram, x1_dram, x2_dram, lap_dram, w_dram, b
         for unit in range(UNITS - 1):
             i, b = divmod(unit, B)
             feat[unit] = three.tile([P, N_TILE, ORDERS], BF16, align_bytes=64, name="feat")
-            split = N_TILE - (64 if unit < 4 else SCALAR_COLS if unit + PASSES < LAP_PASSES else SCALAR_COLS_END)
+            split = N_TILE - (96 if unit < 4 else SCALAR_COLS if unit + PASSES < LAP_PASSES else SCALAR_COLS_END)
             third_term(unit)
             for piece in range(quantised, min(unit + LEAD if unit > 0 else quantised, LAP_PASSES)):
                 quantise_lap_piece(piece)
@@ -343,7 +346,7 @@ def tile_graph_conv_pb_kernel(tc, x0_dram, x1_dram, x2_dram, lap_dram, w_dram, b
                 transposed += 1
             interleave_features(unit, s_copy, slice(split, N_TILE))
             if i + 1 < CHUNKS and b >= 2:
-                term_to_planes("x1", 1, i + 1, b - 2, flip_psum, "flip", False, s_copy)
+                term_to_planes("x1", 1, i + 1, b - 2, flip_psum, "flip", True, s_copy)
             if i == 1 and b < 2:
                 x2_to_planes(PASSES - 1, b)
             if 0 < unit < UNITS - 1:

from contextlib import ExitStack

import concourse.mybir as mybir
from concourse.masks import make_identity

BF16 = mybir.dt.bfloat16
F32 = mybir.dt.float32
U32 = mybir.dt.uint32
U8 = mybir.dt.uint8
FP8X4 = mybir.dt.float8_e4m3fn_x4

P = 128
PACK = 4
K_PASS = P * PACK
N_TILE = 512

B, C, V, ORDERS, OUT = 4, 128, 2048, 4, 128
CB = C * B
CHUNKS = V // N_TILE
PASSES = V // K_PASS
UNITS = CHUNKS * B
LAP_PASSES = CHUNKS * PASSES
LEAD = 5
SCALAR_COLS = 144
SCALAR_COLS_END = 256

FLOPS = 2 * V * V * CB + 2 * B * V * C * ORDERS * OUT


def tile_graph_conv_pb_kernel(tc, x0_dram, x1_dram, x2_dram, lap_dram, w_dram, bias_dram, out_dram):
    nc = tc.nc
    mult = mybir.AluOpType.mult
    subtract = mybir.AluOpType.subtract

    with ExitStack() as ctx:
        keep = ctx.enter_context(tc.tile_pool(name="keep", bufs=1))
        two = ctx.enter_context(tc.tile_pool(name="two", bufs=2))
        eight = ctx.enter_context(tc.tile_pool(name="eight", bufs=8))
        four = ctx.enter_context(tc.tile_pool(name="four", bufs=4))
        three = ctx.enter_context(tc.tile_pool(name="three", bufs=3))
        flip_psum = ctx.enter_context(tc.psum_pool(name="flip", bufs=4))
        acc_psum = ctx.enter_context(tc.psum_pool(name="acc", bufs=2))
        y_psum = ctx.enter_context(tc.psum_pool(name="y", bufs=2))
        ctx.enter_context(tc.manual_schedule())

        ident = keep.tile([P, P], F32)
        make_identity(nc, ident[:])
        ident_half = keep.tile([P, P], BF16)
        nc.vector.tensor_copy(out=ident_half[:], in_=ident[:])
        bias_square = keep.tile([P, P], F32)
        nc.vector.memset(bias_square[:], 0.0)

        term_rows = {"x2": keep.tile([P, CHUNKS * PACK * CB], BF16, name="x2_rows")}
        x1_rows = {}
        term_views = {
            "x1": x1_dram.rearrange("(g s q) w -> g q s w", g=CHUNKS, s=PACK, q=P),
            "x2": x2_dram.rearrange("(g uh q e) w -> g q uh (e w)", g=CHUNKS, uh=2, q=P, e=2),
        }

        def load_term_chunk(name, g):
            if name == "x1":
                x1_rows[g] = two.tile([P, PACK * CB], BF16, name="x1_rows")
                rows = x1_rows[g][:]
            else:
                rows = term_rows[name][:, g * PACK * CB : (g + 1) * PACK * CB]
            nc.sync.dma_start(
                out=rows.rearrange("q (r w) -> q r w", r=term_views[name].shape[2]), in_=term_views[name][g]
            )

        lap_view = lap_dram.rearrange("(i p j) u -> i p j u", i=CHUNKS, p=P, j=PACK)
        lap_rows = {}

        def load_lap_half(i, a):
            if a == 0:
                lap_rows[i] = three.tile([P, PACK, V], BF16, name="lap_rows")
            if i == 0:
                half = slice(a * V // 2, (a + 1) * V // 2)
                nc.sync.dma_start(out=lap_rows[i][:, :, half], in_=lap_view[i][:, :, half])
            else:
                half = slice(a * PACK // 2, (a + 1) * PACK // 2)
                nc.sync.dma_start(
                    out=lap_rows[i][:, half, :].rearrange("p j u -> p (j u)"),
                    in_=lap_view[i][:, half, :].rearrange("p j u -> p (j u)"),
                )

        x0_view = x0_dram.rearrange("b c v -> c b v")
        planes = {}

        for i in range(CHUNKS):
            planes[i] = keep.tile([P, ORDERS, B, N_TILE], BF16, name="planes%d" % i)

        def load_x0_chunk(i):
            nc.sync.dma_start(out=planes[i][:, 0, :, :], in_=x0_view[:, :, i * N_TILE : (i + 1) * N_TILE])

        w_rows = keep.tile([OUT, C * ORDERS], BF16)
        bias_row = keep.tile([1, OUT], BF16)
        for g in range(PASSES):
            load_term_chunk("x2", g)
        load_lap_half(0, 0)
        nc.sync.dma_start(out=bias_row[:], in_=bias_dram.rearrange("(one o) -> one o", one=1))
        nc.sync.dma_start(out=w_rows[:], in_=w_dram)
        load_lap_half(0, 1)
        load_term_chunk("x1", 0)
        load_x0_chunk(0)

        w_codes = keep.tile([P, OUT], U32, align_bytes=64)
        w_scales = keep.tile([P, OUT], U8, align_bytes=64)
        w_grouped = keep.tile([P, OUT * PACK], BF16, align_bytes=64)
        bias_col = keep.tile([P, 1], F32)

        w_flip = {}

        def transpose_weight_and_bias():
            w_words = w_rows[:].bitcast(F32).rearrange("o (c hh) -> o hh c", hh=2)
            flip = flip_psum.tile([P, N_TILE], F32, name="flip")
            for hh in range(2):
                nc.tensor.transpose(flip[:, hh * OUT : (hh + 1) * OUT], w_words[:, hh, :], ident[:])
            nc.tensor.transpose(flip[:, 2 * OUT : 3 * OUT], bias_square[:], ident[:])
            w_flip[0] = flip

        def copy_weight_and_bias():
            flip = w_flip[0]
            nc.vector.tensor_copy(
                out=w_grouped[:].bitcast(F32).rearrange("c (o hh) -> c o hh", hh=2),
                in_=flip[:, 0 : 2 * OUT].rearrange("c (hh o) -> c o hh", hh=2),
            )
            nc.vector.tensor_copy(out=bias_col[:], in_=flip[:, 2 * OUT : 2 * OUT + 1])

        def prepare_weight_and_bias():
            transpose_weight_and_bias()
            copy_weight_and_bias()

        def quantise_weight():
            nc.vector.quantize_mx(out=w_codes[:].bitcast(FP8X4), scales=w_scales[:], in_=w_grouped[:])


        def term_to_planes(name, order, g, h, pool, tag, by_matmul, copy):
            rows = x1_rows[g][:]
            values = rows.rearrange("q (s c b) -> q s b c", s=PACK, c=C)
            flip = pool.tile([P, 2 * N_TILE], BF16, name=tag)
            for eb in range(2):
                for s in range(PACK):
                    slot = eb * PACK + s
                    out = flip[:, slot * P : (slot + 1) * P]
                    in_ = values[:, s, 2 * h + eb, :]
                    if by_matmul:
                        nc.tensor.matmul(out, lhsT=in_, rhs=ident_half[:], start=True, stop=True)
                    else:
                        nc.tensor.transpose(out, in_, ident_half[:])
            copy(
                out=planes[g][:, order, 2 * h : 2 * h + 2, :].rearrange("c eb v -> c (eb v)").bitcast(F32),
                in_=flip[:].bitcast(F32),
            )

        x2_codes = keep.tile([P, PASSES, CB], U32, align_bytes=64)
        x2_scales = keep.tile([P, PASSES, CB], U8, align_bytes=64)
        x2_grouped = {}

        def group_x2(g):
            x2_grouped[g] = two.tile([P, CB * PACK], BF16, align_bytes=64, name="x2_grouped")
            nc.vector.tensor_copy(
                out=x2_grouped[g][:].rearrange("q (b c t) -> q b c t", b=B, c=C),
                in_=term_rows["x2"][:, g * PACK * CB : (g + 1) * PACK * CB].rearrange(
                    "q (t c b) -> q b c t", t=PACK, c=C
                ),
            )

        def x2_to_planes(g, h):
            words = x2_grouped[g][:].bitcast(F32).rearrange("q (b c uh) -> q b uh c", b=B, c=C)
            flip = flip_psum.tile([P, N_TILE], F32, name="flip")
            for eb in range(2):
                for uh in range(2):
                    slot = eb * 2 + uh
                    nc.tensor.transpose(flip[:, slot * P : (slot + 1) * P], words[:, 2 * h + eb, uh, :], ident[:])
            nc.scalar.copy(
                out=planes[g][:, 2, 2 * h : 2 * h + 2, :].rearrange("c eb v -> c (eb v)").bitcast(F32), in_=flip[:]
            )

        def quantise_x2(g):
            nc.vector.quantize_mx(
                out=x2_codes[:, g, :].bitcast(FP8X4), scales=x2_scales[:, g, :], in_=x2_grouped[g][:]
            )

        lap_grouped = {}
        lap_codes = {}
        lap_scales = {}

        def transpose_lap_half(piece, a, copy):
            i, g = divmod(piece, PASSES)
            words = lap_rows[i][:].rearrange("p j u -> p (j u)").bitcast(F32).rearrange("p (j w) -> p j w", j=PACK)
            if a == 0:
                lap_grouped[piece] = four.tile([P, N_TILE * PACK], BF16, align_bytes=64, name="lap_grouped")
            grouped_words = lap_grouped[piece][:].bitcast(F32).rearrange("q (n uh) -> q n uh", uh=2)
            flip = flip_psum.tile([P, N_TILE], F32, name="flip")
            for jl in range(2):
                for uh in range(2):
                    slot = jl * 2 + uh
                    first = (K_PASS // 2) * g + P * uh
                    nc.tensor.transpose(
                        flip[:, slot * P : (slot + 1) * P], words[:, 2 * a + jl, first : first + P], ident[:]
                    )
            copy(
                out=grouped_words[:, 2 * P * a : 2 * P * (a + 1), :].rearrange("q (jl p) uh -> q jl p uh", jl=2),
                in_=flip[:].rearrange("q (jl uh p) -> q jl p uh", jl=2, uh=2),
            )

        def quantise_lap_piece(piece):
            i, g = divmod(piece, PASSES)
            if g == 0:
                lap_codes[i] = two.tile([P, PASSES, N_TILE], U32, align_bytes=64, name="lap_codes")
                lap_scales[i] = two.tile([P, PASSES, N_TILE], U8, align_bytes=64, name="lap_scales")
            nc.vector.quantize_mx(
                out=lap_codes[i][:, g, :].bitcast(FP8X4), scales=lap_scales[i][:, g, :], in_=lap_grouped[piece][:]
            )

        acc = {}
        feat_codes = {}
        feat_scales = {}
        feat = {}

        def first_matmul(unit):
            i, b = divmod(unit, B)
            acc[unit] = acc_psum.tile([P, N_TILE], F32, name="acc")
            for g in range(PASSES):
                nc.tensor.matmul_mx(
                    out=acc[unit][:],
                    lhsT=x2_codes[:, g, b * C : (b + 1) * C].bitcast(FP8X4),
                    lhsT_scale=x2_scales[:, g, b * C : (b + 1) * C],
                    rhs=lap_codes[i][:, g, :].bitcast(FP8X4),
                    rhs_scale=lap_scales[i][:, g, :],
                    start=(g == 0),
                    stop=(g == PASSES - 1),
                )

        def third_term(unit):
            i, b = divmod(unit, B)
            nc.vector.scalar_tensor_tensor(
                out=planes[i][:, 3, b, :].rearrange("c (p j) -> c p j", j=PACK),
                in0=acc[unit][:].rearrange("c (j p) -> c p j", j=PACK),
                scalar=2.0,
                in1=planes[i][:, 1, b, :].rearrange("c (p j) -> c p j", j=PACK),
                op0=mult,
                op1=subtract,
            )

        def interleave_features(unit, copy, cols):
            i, b = divmod(unit, B)
            copy(
                out=feat[unit][:, cols, :].rearrange("c (n r) k -> c n k r", r=8),
                in_=planes[i][:, :, b, cols].rearrange("c k (n r) -> c n k r", r=8),
            )

        def quantise_features(unit, cols=slice(0, N_TILE)):
            if cols.start == 0:
                feat_codes[unit] = three.tile([P, N_TILE], U32, align_bytes=64, name="feat_codes")
                feat_scales[unit] = three.tile([P, N_TILE], U8, align_bytes=64, name="feat_scales")
            nc.vector.quantize_mx(
                out=feat_codes[unit][:, cols].bitcast(FP8X4),
                scales=feat_scales[unit][:, cols],
                in_=feat[unit][:, cols, :].rearrange("c n k -> c (n k)"),
            )

        def second_matmul(unit, cols=slice(0, N_TILE)):
            y = y_psum.tile([P, N_TILE], F32, name="y")
            nc.tensor.matmul_mx(
                out=y[:, cols],
                lhsT=w_codes[:].bitcast(FP8X4),
                lhsT_scale=w_scales[:],
                rhs=feat_codes[unit][:, cols].bitcast(FP8X4),
                rhs_scale=feat_scales[unit][:, cols],
                start=True,
                stop=True,
            )
            return y

        def add_bias_on_scalar(out, y):
            nc.scalar.activation(
                out=out, in_=y, func=mybir.ActivationFunctionType.Identity, bias=bias_col[:, 0:1], scale=1.0
            )

        def add_bias_on_vector(out, y):
            nc.vector.tensor_scalar(out=out, in0=y, scalar1=bias_col[:, 0:1], scalar2=None, op0=mybir.AluOpType.add)

        def store(unit, y, add_bias=add_bias_on_scalar, cols=slice(0, N_TILE)):
            i, b = divmod(unit, B)
            width = cols.stop - cols.start
            y_sb = eight.tile([P, width], F32, name="y_sb%d" % width)
            add_bias(y_sb[:], y[:, cols])
            nc.sync.dma_start(
                out=out_dram[b, :, i * N_TILE + cols.start : i * N_TILE + cols.stop], in_=y_sb[:]
            )

        v_copy = nc.vector.tensor_copy
        s_copy = nc.scalar.copy

        def transpose_lap_piece(piece, copies):
            for a in range(2):
                transpose_lap_half(piece, a, copies[a])

        for g in range(PASSES + 1):
            if g < PASSES:
                group_x2(g)
                if g < 3:
                    for h in range(2):
                        x2_to_planes(g, h)
            if g > 0:
                quantise_x2(g - 1)

        for i in range(1, CHUNKS):
            load_lap_half(i, 0)
            load_lap_half(i, 1)
            load_term_chunk("x1", i)
            load_x0_chunk(i)

        nc.vector.tensor_copy(out=bias_square[0:1, :], in_=bias_row[:])
        for piece in range(PASSES):
            if piece == 2:
                prepare_weight_and_bias()
                quantise_weight()
            transpose_lap_piece(piece, (s_copy, (s_copy, v_copy)[piece % 2]))
            if piece > 0:
                quantise_lap_piece(piece - 1)
        quantise_lap_piece(PASSES - 1)
        term_to_planes("x1", 1, 0, 0, y_psum, "y", True, s_copy)
        first_matmul(0)
        term_to_planes("x1", 1, 0, 1, y_psum, "y", True, s_copy)
        first_matmul(1)
        transpose_lap_piece(PASSES, (s_copy, s_copy))
        transposed = PASSES + 1
        quantised = PASSES


        y = {}
        for unit in range(UNITS - 1):
            i, b = divmod(unit, B)
            feat[unit] = three.tile([P, N_TILE, ORDERS], BF16, align_bytes=64, name="feat")
            split = N_TILE - (96 if unit < 4 else SCALAR_COLS if unit + PASSES < LAP_PASSES else SCALAR_COLS_END)
            third_term(unit)
            for piece in range(quantised, min(unit + LEAD if unit > 0 else quantised, LAP_PASSES)):
                quantise_lap_piece(piece)
                quantised += 1
            if unit > 0:
                quantise_features(unit - 1)
            for piece in range(transposed, min(unit + LEAD + 1, LAP_PASSES)):
                transpose_lap_piece(piece, (s_copy, s_copy))
                transposed += 1
            interleave_features(unit, s_copy, slice(split, N_TILE))
            if i + 1 < CHUNKS and b >= 2:
                term_to_planes("x1", 1, i + 1, b - 2, flip_psum, "flip", True, s_copy)
            if i == 1 and b < 2:
                x2_to_planes(PASSES - 1, b)
            if 0 < unit < UNITS - 1:
                first_matmul(unit + 1)
            if unit >= 2:
                y[unit - 2] = second_matmul(unit - 2)
            if unit >= 2:
                store(unit - 2, y[unit - 2])
            interleave_features(unit, v_copy, slice(0, split))

        last = UNITS - 1
        half = N_TILE // 2
        third_term(last)
        quantise_features(last - 1)
        y[last - 2] = second_matmul(last - 2)
        feat[last] = three.tile([P, N_TILE, ORDERS], BF16, align_bytes=64, name="feat")
        interleave_features(last, s_copy, slice(N_TILE - 128, N_TILE))
        store(last - 2, y[last - 2])
        interleave_features(last, v_copy, slice(0, half))
        interleave_features(last, v_copy, slice(half, N_TILE - 128))
        y[last - 1] = second_matmul(last - 1)
        store(last - 1, y[last - 1])
        for cols, add_bias in ((slice(0, half), add_bias_on_scalar), (slice(half, N_TILE), add_bias_on_vector)):
            quantise_features(last, cols)
            store(last, second_matmul(last, cols), add_bias, cols)
